import numpy as np
import ml_dtypes


def mxq(x, axis, fmt="e4m3"):
    dtype, down = {"e4m3": (ml_dtypes.float8_e4m3fn, 7), "e5m2": (ml_dtypes.float8_e5m2, 14)}[fmt]
    v = np.moveaxis(np.asarray(x, np.float32).astype(ml_dtypes.bfloat16).astype(np.float64), axis, -1)
    blocks = v.reshape(v.shape[:-1] + (-1, 32))
    amax = np.abs(blocks).max(-1, keepdims=True)
    byte = np.maximum(np.where(amax > 0, np.frexp(amax)[1] - 1 + 127, 0) - down, 1)
    scale = np.exp2(byte - 127.0)
    codes = (blocks / scale).astype(np.float32).astype(dtype).astype(np.float64)
    return np.moveaxis((codes * scale).reshape(v.shape), -1, axis)


WIDE = False


def mx_kscale(k):
    if not WIDE:
        return np.ones(k)
    levels = np.array([10, -10, 5, -5, 0])
    a = np.random.permutation(np.resize(levels, k // 512 * 4)).reshape(k // 512, 4)
    idx = np.arange(k)
    return np.exp2(a[idx // 512, idx % 128 // 32])


BF16 = ml_dtypes.bfloat16


def bf(x):
    return np.asarray(x, np.float32).astype(BF16)


def f64(x):
    return np.asarray(x).astype(np.float64)


B, H, W, C, NH, WS, SHIFT, F = 4, 32, 32, 512, 16, 8, 3, 512
S = WS * WS
HD = C // NH
NWIN = B * (H // WS) * (W // WS)
EPS = 1e-5


def layer_norm(x, w, b):
    m = x.mean(-1, keepdims=True)
    v = ((x - m) ** 2).mean(-1, keepdims=True)
    return (x - m) / np.sqrt(v + EPS) * w + b


def erf(z):
    a = np.clip(z, -6.0, 6.0)
    t2 = 2.0 * a * a
    term = a.copy()
    tot = a.copy()
    for n in range(1, 110):
        term = term * t2 / (2 * n + 1)
        tot = tot + term
    return 2.0 / np.sqrt(np.pi) * np.exp(-a * a) * tot


def gelu(v):
    return 0.5 * v * (1.0 + erf(v / np.sqrt(2.0)))


def setup_inputs():
    s = mx_kscale(C)
    t = mx_kscale(C)
    return {"o_heads": bf(0.25 * np.random.standard_normal((NWIN, NH, S, HD)) * s.reshape(NH, 1, HD)),
            "x": bf(np.random.standard_normal((B, H * W, C))),
            "out_w": bf(2.0 * np.random.standard_normal((C, C)) / np.sqrt(C) / s[None, :]),
            "out_b": bf(0.1 * np.random.standard_normal(C)),
            "norm2_w": bf((1.0 + 0.1 * np.random.standard_normal(C)) * t),
            "norm2_b": bf(0.1 * np.random.standard_normal(C) * t),
            "fc1_w": bf(np.random.standard_normal((F, C)) / np.sqrt(C) / t[None, :]),
            "fc1_b": bf(0.1 * np.random.standard_normal(F))}


def reference(o_heads, x, out_w, out_b, norm2_w, norm2_b, fc1_w, fc1_b):
    o = f64(o_heads).transpose(0, 2, 1, 3).reshape(-1, S, C)
    o = (mxq(o, 2, "e4m3") @ mxq(f64(out_w), 1, "e4m3").T) + f64(out_b)
    o = o.reshape(B, H // WS, W // WS, WS, WS, C)
    o = o.transpose(0, 1, 3, 2, 4, 5).reshape(B, H, W, C)
    o = np.roll(o, (SHIFT, SHIFT), axis=(1, 2))
    x2 = f64(x) + o.reshape(B, H * W, C)
    h2 = layer_norm(x2, f64(norm2_w), f64(norm2_b))
    g = gelu((mxq(h2, 2, "e4m3") @ mxq(f64(fc1_w), 1, "e4m3").T) + f64(fc1_b))
    return x2, g

@@ -1,0 +1,313 @@
+from contextlib import ExitStack
+
+import concourse.mybir as mybir
+from concourse.masks import make_identity
+
+F32 = mybir.dt.float32
+BF16 = mybir.dt.bfloat16
+U32 = mybir.dt.uint32
+U8 = mybir.dt.uint8
+FP8X4 = mybir.dt.float8_e4m3fn_x4
+ALU = mybir.AluOpType
+ACT = mybir.ActivationFunctionType
+
+P = 128
+IMAGES = 4
+CH = 512
+HEADS = 16
+HEAD_DIM = 32
+WIN = 8
+WINDOWS = 16
+SHIFT = 3
+RUN = 8
+GROUP = 4
+HALVES = RUN // GROUP
+GROUPS = IMAGES * HALVES
+EPS = 1e-5
+
+FLOPS = 2 * 2 * IMAGES * 1024 * CH * CH
+
+
+def tile_swintransformerblock_pb_t_kernel(
+    tc, o_heads, x, out_w, out_b, norm2_w, norm2_b, fc1_w, fc1_b, out_0, out_1
+):
+    nc = tc.nc
+    with ExitStack() as pools:
+        consts = pools.enter_context(tc.tile_pool(name="consts", bufs=1))
+        inputs = pools.enter_context(tc.tile_pool(name="inputs", bufs=1))
+        stage = pools.enter_context(tc.tile_pool(name="stage", bufs=2))
+        rows4 = pools.enter_context(tc.tile_pool(name="rows4", bufs=4))
+        stats = pools.enter_context(tc.tile_pool(name="stats", bufs=3))
+        psum_word = pools.enter_context(tc.psum_pool(name="psum_word", bufs=2))
+        psum_chan = pools.enter_context(tc.psum_pool(name="psum_chan", bufs=4))
+        psum_acc = pools.enter_context(tc.psum_pool(name="psum_acc", bufs=2))
+        pools.enter_context(tc.manual_schedule())
+
+        heads_of = {}
+        x_of = {}
+
+        def load_image(b):
+            heads = inputs.tile([P, HEADS, WIN * HEAD_DIM], BF16, name="heads%d" % b)
+            for a in range(HEADS):
+                nc.sync.dma_start(
+                    out=heads[:, a, :],
+                    in_=o_heads[WINDOWS * b : WINDOWS * (b + 1), a].rearrange(
+                        "n (r c) d -> n r (c d)", c=WIN
+                    ),
+                )
+            heads_of[b] = heads
+            x_sb = inputs.tile([P, RUN, CH], BF16, name="x%d" % b)
+            nc.sync.dma_start(out=x_sb[:], in_=x[b].rearrange("(p u) c -> p u c", u=RUN))
+            x_of[b] = x_sb
+
+        norm_rows = consts.tile([P, P], BF16)
+        nc.vector.memset(norm_rows[:], 0.0)
+
+        out_w_sb = consts.tile([P, 4, CH], BF16)
+        nc.sync.dma_start(out=out_w_sb[:], in_=out_w.rearrange("(o p) k -> p o k", p=P))
+        out_b_bc = consts.tile([P, CH], BF16)
+        nc.sync.dma_start(out=out_b_bc[:], in_=out_b.partition_broadcast(P))
+        load_image(0)
+        fc1_w_sb = consts.tile([P, 4, CH], BF16)
+        nc.sync.dma_start(out=fc1_w_sb[:], in_=fc1_w.rearrange("(o p) k -> p o k", p=P))
+        nc.sync.dma_start(out=norm_rows[0:4, :], in_=norm2_w.rearrange("(t p) -> t p", p=P))
+        nc.sync.dma_start(out=norm_rows[4:8, :], in_=norm2_b.rearrange("(t p) -> t p", p=P))
+        fc1_b_bc = consts.tile([P, CH], BF16)
+        nc.sync.dma_start(out=fc1_b_bc[:], in_=fc1_b.partition_broadcast(P))
+        for b in range(1, IMAGES):
+            load_image(b)
+
+        ident_f32 = consts.tile([P, P], F32)
+        make_identity(nc, ident_f32[:])
+        ident_bf16 = consts.tile([P, P], BF16)
+        make_identity(nc, ident_bf16[:])
+
+        row_major = consts.tile([P, P], F32)
+        nc.vector.tensor_copy(
+            out=row_major[:].rearrange("k (wi r wj) -> k wi r wj", wi=4, r=WIN),
+            in_=ident_f32[:].rearrange("k (wi wj r) -> k wi r wj", wi=4, wj=4),
+        )
+        perm_plain = consts.tile([P, P], F32)
+        roll = 4 * SHIFT
+        nc.vector.tensor_copy(out=perm_plain[:, roll:P], in_=row_major[:, 0 : P - roll])
+        nc.vector.tensor_copy(out=perm_plain[:, 0:roll], in_=row_major[:, P - roll : P])
+        perm_carry = consts.tile([P, P], F32)
+        plain_v = perm_plain[:].rearrange("k (i q) -> k i q", q=4)
+        carry_v = perm_carry[:].rearrange("k (i q) -> k i q", q=4)
+        nc.vector.tensor_copy(out=carry_v[:, :, 1:4], in_=plain_v[:, :, 0:3])
+        nc.vector.tensor_copy(out=carry_v[:, :, 0:1], in_=plain_v[:, :, 3:4])
+
+        minus_half = consts.tile([P, GROUP], F32)
+        nc.vector.memset(minus_half[:], -0.5)
+        ones4 = consts.tile([P, 4], F32)
+        nc.vector.memset(ones4[:], 1.0)
+        zeros4 = consts.tile([P, 4], F32)
+        nc.vector.memset(zeros4[:], 0.0)
+        norm_cols = consts.tile([P, 8], F32)
+
+        def quantise(grouped, pool, tag):
+            codes = pool.tile([P, GROUP * P], U32, tag=tag + "_codes", name=tag + "_codes", align_bytes=64)
+            scales = pool.tile([P, GROUP * P], U8, tag=tag + "_scales", name=tag + "_scales", align_bytes=64)
+            nc.vector.quantize_mx(out=codes[:].bitcast(FP8X4), scales=scales[:], in_=grouped)
+            return codes, scales
+
+        def transpose_words(words_of, perm_of):
+            grouped = stage.tile([P, GROUP * P * 4], BF16, tag="grouped_w", align_bytes=64)
+            grouped_words = grouped[:].bitcast(F32).rearrange("w (n h) -> w n h", h=2)
+            for pair in range(GROUP // 2):
+                bank = psum_word.tile([P, 2, 2, P], F32, tag="word_bank")
+                for h in range(2):
+                    for jj in range(2):
+                        j = 2 * pair + jj
+                        nc.tensor.transpose(
+                            bank[:, h, jj, :], words_of(j)[:, P * h : P * (h + 1)], perm_of(j)
+                        )
+                nc.scalar.copy(
+                    out=grouped_words[:, 2 * P * pair : 2 * P * (pair + 1), :],
+                    in_=bank[:].rearrange("w h j n -> w (j n) h"),
+                )
+            return grouped
+
+        def transpose_channel_blocks(rows, gain, beta):
+            planes = stage.tile([P, 4, GROUP * P], BF16, tag="planes")
+            for t in range(4):
+                bank = psum_chan.tile([P, GROUP, P], F32, tag="chan_bank")
+                for j in range(GROUP):
+                    nc.tensor.transpose(bank[:, j, :], rows[:, j, P * t : P * (t + 1)], ident_f32[:])
+                nc.scalar.activation(
+                    out=planes[:, t, :],
+                    in_=bank[:].rearrange("p j n -> p (j n)"),
+                    func=ACT.Identity,
+                    scale=gain[:, t : t + 1],
+                    bias=beta[:, t : t + 1],
+                )
+            return planes
+
+        def quantise_planes(planes, pool, tag):
+            grouped = stage.tile([P, GROUP * P, 4], BF16, tag="grouped_c", align_bytes=64)
+            nc.vector.tensor_copy(out=grouped[:], in_=planes[:].rearrange("p t n -> p n t"))
+            return quantise(grouped[:].rearrange("p n t -> p (n t)"), pool, tag)
+
+        regrouped_of = {}
+        grouped_m_of = {}
+        m_of = {}
+        x2_of = {}
+        mean_of = {}
+        rstd_of = {}
+        planes_of = {}
+        h_of = {}
+
+        def regroup_heads(g):
+            b, half = divmod(g, HALVES)
+            if half == 0:
+                regrouped = stage.tile([P, WIN, CH], BF16, tag="regrouped")
+                nc.vector.tensor_copy(
+                    out=regrouped[:].rearrange("p c (a d) -> p c a d", d=HEAD_DIM),
+                    in_=heads_of[b][:].rearrange("p a (c d) -> p c a d", d=HEAD_DIM),
+                )
+                regrouped_of[b] = regrouped
+
+        def transpose_heads(g):
+            b, half = divmod(g, HALVES)
+            words = regrouped_of[b][:].bitcast(F32)
+            grouped_m_of[g] = transpose_words(
+                lambda j: words[:, (GROUP * half + j - SHIFT) % WIN, :],
+                lambda j: perm_carry[:] if GROUP * half + j < SHIFT else perm_plain[:],
+            )
+
+        def add_bias_to_x(g):
+            b, half = divmod(g, HALVES)
+            x2 = rows4.tile([P, GROUP, CH], F32, tag="x2")
+            for j in range(GROUP):
+                nc.gpsimd.tensor_tensor(
+                    out=x2[:, j, :], in0=x_of[b][:, GROUP * half + j, :], in1=out_b_bc[:], op=ALU.add
+                )
+            x2_of[g] = x2
+
+        def project(g):
+            b, half = divmod(g, HALVES)
+            codes, scales = m_of[g]
+            x2 = x2_of[g]
+            row_sum = stats.tile([P, GROUP], F32, tag="row_sum")
+            squares = stage.tile([P, GROUP, CH], BF16, tag="squares")
+            sq_sum = stats.tile([P, GROUP], F32, tag="sq_sum")
+            for j in range(GROUP):
+                cols = slice(P * j, P * (j + 1))
+                acc = psum_acc.tile([P, CH], F32, tag="acc")
+                nc.tensor.matmul_mx(
+                    out=acc[:],
+                    lhsT=codes[:, cols].bitcast(FP8X4),
+                    lhsT_scale=scales[:, cols],
+                    rhs=out_w_codes[:].bitcast(FP8X4),
+                    rhs_scale=out_w_scales[:],
+                    start=True,
+                    stop=True,
+                )
+                nc.vector.scalar_tensor_tensor(
+                    out=x2[:, j, :],
+                    in0=acc[:],
+                    scalar=1.0,
+                    in1=x2[:, j, :],
+                    op0=ALU.mult,
+                    op1=ALU.add,
+                    accum_out=row_sum[:, j : j + 1],
+                )
+                nc.scalar.activation(
+                    out=squares[:, j, :],
+                    in_=x2[:, j, :],
+                    func=ACT.Square,
+                    bias=row_sum[:, j : j + 1],
+                    scale=-1.0 * CH,
+                    accum_out=sq_sum[:, j : j + 1],
+                )
+            nc.sync.dma_start(
+                out=out_0[b].rearrange("(p u) c -> p u c", u=RUN)[:, GROUP * half : GROUP * (half + 1), :],
+                in_=x2[:],
+            )
+            neg_mean = stats.tile([P, GROUP], F32, tag="neg_mean")
+            nc.gpsimd.tensor_scalar(
+                out=neg_mean[:], in0=row_sum[:], scalar1=-1.0 / CH, scalar2=0.0, op0=ALU.mult, op1=ALU.add
+            )
+            var_eps = stats.tile([P, GROUP], F32, tag="var_eps")
+            nc.gpsimd.tensor_scalar(
+                out=var_eps[:], in0=sq_sum[:], scalar1=1.0 / CH**3, scalar2=EPS, op0=ALU.mult, op1=ALU.add
+            )
+            rstd = stats.tile([P, GROUP], F32, tag="rstd")
+            nc.gpsimd.tensor_tensor(out=rstd[:], in0=var_eps[:], in1=minus_half[:], op=ALU.pow)
+            mean_of[g] = neg_mean
+            rstd_of[g] = rstd
+
+        def spread(g):
+            rows = stage.tile([P, GROUP, CH], F32, tag="rows")
+            if g < 0:
+                norm_bank = psum_word.tile([P, P], BF16, tag="word_bank")
+                nc.tensor.transpose(norm_bank[:], norm_rows[:], ident_bf16[:])
+                nc.vector.tensor_copy(out=norm_cols[:], in_=norm_bank[:, 0:8])
+                nc.vector.tensor_copy(out=rows[:], in_=fc1_w_sb[:])
+                planes_of[g] = transpose_channel_blocks(rows, ones4, zeros4)
+            else:
+                for j in range(GROUP):
+                    nc.vector.tensor_scalar(
+                        out=rows[:, j, :],
+                        in0=x2_of[g][:, j, :],
+                        scalar1=mean_of[g][:, j : j + 1],
+                        scalar2=rstd_of[g][:, j : j + 1],
+                        op0=ALU.add,
+                        op1=ALU.mult,
+                    )
+                planes_of[g] = transpose_channel_blocks(rows, norm_cols[:, 0:4], norm_cols[:, 4:8])
+
+        def pack(g):
+            if g < 0:
+                h_of[g] = quantise_planes(planes_of[g], consts, "fc1_w")
+            else:
+                h_of[g] = quantise_planes(planes_of[g], stage, "h")
+
+        def mlp(g):
+            b, half = divmod(g, HALVES)
+            codes, scales = h_of[g]
+            fc1_w_codes, fc1_w_scales = h_of[-1]
+            gel = stage.tile([P, GROUP, CH], F32, tag="gel")
+            for j in range(GROUP):
+                cols = slice(P * j, P * (j + 1))
+                acc = psum_acc.tile([P, CH], F32, tag="acc")
+                nc.tensor.matmul_mx(
+                    out=acc[:],
+                    lhsT=codes[:, cols].bitcast(FP8X4),
+                    lhsT_scale=scales[:, cols],
+                    rhs=fc1_w_codes[:].bitcast(FP8X4),
+                    rhs_scale=fc1_w_scales[:],
+                    start=True,
+                    stop=True,
+                )
+                nc.vector.tensor_tensor(out=gel[:, j, :], in0=acc[:], in1=fc1_b_bc[:], op=ALU.add)
+                nc.scalar.activation(out=gel[:, j, :], in_=gel[:, j, :], func=ACT.Gelu)
+            nc.sync.dma_start(
+                out=out_1[b].rearrange("(p u) c -> p u c", u=RUN)[:, GROUP * half : GROUP * (half + 1), :],
+                in_=gel[:],
+            )
+
+        out_w_words = out_w_sb[:].bitcast(F32)
+        out_w_codes, out_w_scales = quantise(
+            transpose_words(lambda j: out_w_words[:, j, :], lambda j: ident_f32[:])[:], consts, "out_w"
+        )
+
+        def live(g):
+            return 0 <= g < GROUPS
+
+        for step in range(-2, GROUPS + 3):
+            if live(step + 1):
+                transpose_heads(step + 1)
+                add_bias_to_x(step + 1)
+            if live(step):
+                project(step)
+            if live(step - 3):
+                mlp(step - 3)
+            if -1 <= step - 1 < GROUPS:
+                spread(step - 1)
+            if -1 <= step - 2 < GROUPS:
+                pack(step - 2)
+            if live(step + 1):
+                m_of[step + 1] = quantise(grouped_m_of[step + 1][:], stage, "m")
+            if live(step + 2):
+                regroup_heads(step + 2)

@@ -178,10 +178,12 @@ def tile_swintransformerblock_pb_t_kernel(
         def add_bias_to_x(g):
             b, half = divmod(g, HALVES)
             x2 = rows4.tile([P, GROUP, CH], F32, tag="x2")
-            for j in range(GROUP):
-                nc.gpsimd.tensor_tensor(
-                    out=x2[:, j, :], in0=x_of[b][:, GROUP * half + j, :], in1=out_b_bc[:], op=ALU.add
-                )
+            nc.vector.tensor_tensor(
+                out=x2[:],
+                in0=x_of[b][:, GROUP * half : GROUP * (half + 1), :],
+                in1=out_b_bc[:].unsqueeze(1).to_broadcast([P, GROUP, CH]),
+                op=ALU.add,
+            )
             x2_of[g] = x2
 
         def project(g):
@@ -296,18 +298,18 @@ def tile_swintransformerblock_pb_t_kernel(
             return 0 <= g < GROUPS
 
         for step in range(-2, GROUPS + 3):
-            if live(step + 1):
-                transpose_heads(step + 1)
-                add_bias_to_x(step + 1)
             if live(step):
                 project(step)
-            if live(step - 3):
-                mlp(step - 3)
+            if live(step + 1):
+                transpose_heads(step + 1)
             if -1 <= step - 1 < GROUPS:
                 spread(step - 1)
             if -1 <= step - 2 < GROUPS:
                 pack(step - 2)
+            if live(step - 3):
+                mlp(step - 3)
             if live(step + 1):
                 m_of[step + 1] = quantise(grouped_m_of[step + 1][:], stage, "m")
+                add_bias_to_x(step + 1)
             if live(step + 2):
                 regroup_heads(step + 2)

@@ -39,8 +39,8 @@ def tile_swintransformerblock_pb_t_kernel(
         rows4 = pools.enter_context(tc.tile_pool(name="rows4", bufs=4))
         stats = pools.enter_context(tc.tile_pool(name="stats", bufs=3))
         psum_word = pools.enter_context(tc.psum_pool(name="psum_word", bufs=2))
-        psum_chan = pools.enter_context(tc.psum_pool(name="psum_chan", bufs=4))
-        psum_acc = pools.enter_context(tc.psum_pool(name="psum_acc", bufs=2))
+        psum_chan = pools.enter_context(tc.psum_pool(name="psum_chan", bufs=2))
+        psum_acc = pools.enter_context(tc.psum_pool(name="psum_acc", bufs=4))
         pools.enter_context(tc.manual_schedule())
 
         heads_of = {}
@@ -156,6 +156,8 @@ def tile_swintransformerblock_pb_t_kernel(
         rstd_of = {}
         planes_of = {}
         h_of = {}
+        p_of = {}
+        f_of = {}
 
         def regroup_heads(g):
             b, half = divmod(g, HALVES)
@@ -178,21 +180,16 @@ def tile_swintransformerblock_pb_t_kernel(
         def add_bias_to_x(g):
             b, half = divmod(g, HALVES)
             x2 = rows4.tile([P, GROUP, CH], F32, tag="x2")
-            nc.vector.tensor_tensor(
-                out=x2[:],
-                in0=x_of[b][:, GROUP * half : GROUP * (half + 1), :],
-                in1=out_b_bc[:].unsqueeze(1).to_broadcast([P, GROUP, CH]),
-                op=ALU.add,
-            )
+            for j in range(GROUP):
+                nc.gpsimd.tensor_tensor(
+                    out=x2[:, j, :], in0=x_of[b][:, GROUP * half + j, :], in1=out_b_bc[:], op=ALU.add
+                )
             x2_of[g] = x2
 
-        def project(g):
-            b, half = divmod(g, HALVES)
-            codes, scales = m_of[g]
-            x2 = x2_of[g]
-            row_sum = stats.tile([P, GROUP], F32, tag="row_sum")
-            squares = stage.tile([P, GROUP, CH], BF16, tag="squares")
-            sq_sum = stats.tile([P, GROUP], F32, tag="sq_sum")
+        def multiply(tokens, weights):
+            codes, scales = tokens
+            w_codes, w_scales = weights
+            banks = []
             for j in range(GROUP):
                 cols = slice(P * j, P * (j + 1))
                 acc = psum_acc.tile([P, CH], F32, tag="acc")
@@ -200,14 +197,24 @@ def tile_swintransformerblock_pb_t_kernel(
                     out=acc[:],
                     lhsT=codes[:, cols].bitcast(FP8X4),
                     lhsT_scale=scales[:, cols],
-                    rhs=out_w_codes[:].bitcast(FP8X4),
-                    rhs_scale=out_w_scales[:],
+                    rhs=w_codes[:].bitcast(FP8X4),
+                    rhs_scale=w_scales[:],
                     start=True,
                     stop=True,
                 )
+                banks.append(acc)
+            return banks
+
+        def residual(g):
+            b, half = divmod(g, HALVES)
+            x2 = x2_of[g]
+            row_sum = stats.tile([P, GROUP], F32, tag="row_sum")
+            squares = stage.tile([P, GROUP, CH], BF16, tag="squares")
+            sq_sum = stats.tile([P, GROUP], F32, tag="sq_sum")
+            for j in range(GROUP):
                 nc.vector.scalar_tensor_tensor(
                     out=x2[:, j, :],
-                    in0=acc[:],
+                    in0=p_of[g][j][:],
                     scalar=1.0,
                     in1=x2[:, j, :],
                     op0=ALU.mult,
@@ -265,24 +272,11 @@ def tile_swintransformerblock_pb_t_kernel(
             else:
                 h_of[g] = quantise_planes(planes_of[g], stage, "h")
 
-        def mlp(g):
+        def gelu(g):
             b, half = divmod(g, HALVES)
-            codes, scales = h_of[g]
-            fc1_w_codes, fc1_w_scales = h_of[-1]
             gel = stage.tile([P, GROUP, CH], F32, tag="gel")
             for j in range(GROUP):
-                cols = slice(P * j, P * (j + 1))
-                acc = psum_acc.tile([P, CH], F32, tag="acc")
-                nc.tensor.matmul_mx(
-                    out=acc[:],
-                    lhsT=codes[:, cols].bitcast(FP8X4),
-                    lhsT_scale=scales[:, cols],
-                    rhs=fc1_w_codes[:].bitcast(FP8X4),
-                    rhs_scale=fc1_w_scales[:],
-                    start=True,
-                    stop=True,
-                )
-                nc.vector.tensor_tensor(out=gel[:, j, :], in0=acc[:], in1=fc1_b_bc[:], op=ALU.add)
+                nc.vector.tensor_tensor(out=gel[:, j, :], in0=f_of[g][j][:], in1=fc1_b_bc[:], op=ALU.add)
                 nc.scalar.activation(out=gel[:, j, :], in_=gel[:, j, :], func=ACT.Gelu)
             nc.sync.dma_start(
                 out=out_1[b].rearrange("(p u) c -> p u c", u=RUN)[:, GROUP * half : GROUP * (half + 1), :],
@@ -290,26 +284,31 @@ def tile_swintransformerblock_pb_t_kernel(
             )
 
         out_w_words = out_w_sb[:].bitcast(F32)
-        out_w_codes, out_w_scales = quantise(
+        out_w_packed = quantise(
             transpose_words(lambda j: out_w_words[:, j, :], lambda j: ident_f32[:])[:], consts, "out_w"
         )
 
         def live(g):
             return 0 <= g < GROUPS
 
-        for step in range(-2, GROUPS + 3):
-            if live(step):
-                project(step)
+        for step in range(-3, GROUPS + 3):
             if live(step + 1):
-                transpose_heads(step + 1)
+                add_bias_to_x(step + 1)
+            if live(step):
+                residual(step)
+            if live(step - 3):
+                f_of[step - 3] = multiply(h_of[step - 3], h_of[-1])
+            if live(step + 2):
+                transpose_heads(step + 2)
             if -1 <= step - 1 < GROUPS:
                 spread(step - 1)
             if -1 <= step - 2 < GROUPS:
                 pack(step - 2)
-            if live(step - 3):
-                mlp(step - 3)
             if live(step + 1):
                 m_of[step + 1] = quantise(grouped_m_of[step + 1][:], stage, "m")
-                add_bias_to_x(step + 1)
-            if live(step + 2):
-                regroup_heads(step + 2)
+            if live(step - 3):
+                gelu(step - 3)
+            if live(step + 1):
+                p_of[step + 1] = multiply(m_of[step + 1], out_w_packed)
+            if live(step + 3):
+                regroup_heads(step + 3)

@@ -36,7 +36,7 @@ def tile_swintransformerblock_pb_t_kernel(
         consts = pools.enter_context(tc.tile_pool(name="consts", bufs=1))
         inputs = pools.enter_context(tc.tile_pool(name="inputs", bufs=1))
         stage = pools.enter_context(tc.tile_pool(name="stage", bufs=2))
-        rows4 = pools.enter_context(tc.tile_pool(name="rows4", bufs=4))
+        rows4 = pools.enter_context(tc.tile_pool(name="rows4", bufs=5))
         stats = pools.enter_context(tc.tile_pool(name="stats", bufs=3))
         psum_word = pools.enter_context(tc.psum_pool(name="psum_word", bufs=2))
         psum_chan = pools.enter_context(tc.psum_pool(name="psum_chan", bufs=2))
@@ -180,10 +180,12 @@ def tile_swintransformerblock_pb_t_kernel(
         def add_bias_to_x(g):
             b, half = divmod(g, HALVES)
             x2 = rows4.tile([P, GROUP, CH], F32, tag="x2")
-            for j in range(GROUP):
-                nc.gpsimd.tensor_tensor(
-                    out=x2[:, j, :], in0=x_of[b][:, GROUP * half + j, :], in1=out_b_bc[:], op=ALU.add
-                )
+            nc.vector.tensor_tensor(
+                out=x2[:],
+                in0=x_of[b][:, GROUP * half : GROUP * (half + 1), :],
+                in1=out_b_bc[:].unsqueeze(1).to_broadcast([P, GROUP, CH]),
+                op=ALU.add,
+            )
             x2_of[g] = x2
 
         def multiply(tokens, weights):
@@ -292,8 +294,6 @@ def tile_swintransformerblock_pb_t_kernel(
             return 0 <= g < GROUPS
 
         for step in range(-3, GROUPS + 3):
-            if live(step + 1):
-                add_bias_to_x(step + 1)
             if live(step):
                 residual(step)
             if live(step - 3):
@@ -302,6 +302,8 @@ def tile_swintransformerblock_pb_t_kernel(
                 transpose_heads(step + 2)
             if -1 <= step - 1 < GROUPS:
                 spread(step - 1)
+            if live(step + 2):
+                add_bias_to_x(step + 2)
             if -1 <= step - 2 < GROUPS:
                 pack(step - 2)
             if live(step + 1):

@@ -38,8 +38,7 @@ def tile_swintransformerblock_pb_t_kernel(
         stage = pools.enter_context(tc.tile_pool(name="stage", bufs=2))
         rows4 = pools.enter_context(tc.tile_pool(name="rows4", bufs=5))
         stats = pools.enter_context(tc.tile_pool(name="stats", bufs=3))
-        psum_word = pools.enter_context(tc.psum_pool(name="psum_word", bufs=2))
-        psum_chan = pools.enter_context(tc.psum_pool(name="psum_chan", bufs=2))
+        psum_t = pools.enter_context(tc.psum_pool(name="psum_t", bufs=4))
         psum_acc = pools.enter_context(tc.psum_pool(name="psum_acc", bufs=4))
         pools.enter_context(tc.manual_schedule())
 
@@ -62,18 +61,18 @@ def tile_swintransformerblock_pb_t_kernel(
 
         norm_rows = consts.tile([P, P], BF16)
         nc.vector.memset(norm_rows[:], 0.0)
+        bias_rows = consts.tile([P, 2, CH], BF16)
+        nc.vector.memset(bias_rows[:], 0.0)
+        nc.sync.dma_start(out=bias_rows[0:1, 0, :], in_=out_b.unsqueeze(0))
+        nc.sync.dma_start(out=bias_rows[0:1, 1, :], in_=fc1_b.unsqueeze(0))
 
         out_w_sb = consts.tile([P, 4, CH], BF16)
         nc.sync.dma_start(out=out_w_sb[:], in_=out_w.rearrange("(o p) k -> p o k", p=P))
-        out_b_bc = consts.tile([P, CH], BF16)
-        nc.sync.dma_start(out=out_b_bc[:], in_=out_b.partition_broadcast(P))
         load_image(0)
         fc1_w_sb = consts.tile([P, 4, CH], BF16)
         nc.sync.dma_start(out=fc1_w_sb[:], in_=fc1_w.rearrange("(o p) k -> p o k", p=P))
         nc.sync.dma_start(out=norm_rows[0:4, :], in_=norm2_w.rearrange("(t p) -> t p", p=P))
         nc.sync.dma_start(out=norm_rows[4:8, :], in_=norm2_b.rearrange("(t p) -> t p", p=P))
-        fc1_b_bc = consts.tile([P, CH], BF16)
-        nc.sync.dma_start(out=fc1_b_bc[:], in_=fc1_b.partition_broadcast(P))
         for b in range(1, IMAGES):
             load_image(b)
 
@@ -115,7 +114,7 @@ def tile_swintransformerblock_pb_t_kernel(
             grouped = stage.tile([P, GROUP * P * 4], BF16, tag="grouped_w", align_bytes=64)
             grouped_words = grouped[:].bitcast(F32).rearrange("w (n h) -> w n h", h=2)
             for pair in range(GROUP // 2):
-                bank = psum_word.tile([P, 2, 2, P], F32, tag="word_bank")
+                bank = psum_t.tile([P, 2, 2, P], F32, tag="t_bank")
                 for h in range(2):
                     for jj in range(2):
                         j = 2 * pair + jj
@@ -131,7 +130,7 @@ def tile_swintransformerblock_pb_t_kernel(
         def transpose_channel_blocks(rows, gain, beta):
             planes = stage.tile([P, 4, GROUP * P], BF16, tag="planes")
             for t in range(4):
-                bank = psum_chan.tile([P, GROUP, P], F32, tag="chan_bank")
+                bank = psum_t.tile([P, GROUP, P], F32, tag="t_bank")
                 for j in range(GROUP):
                     nc.tensor.transpose(bank[:, j, :], rows[:, j, P * t : P * (t + 1)], ident_f32[:])
                 nc.scalar.activation(
@@ -143,10 +142,13 @@ def tile_swintransformerblock_pb_t_kernel(
                 )
             return planes
 
-        def quantise_planes(planes, pool, tag):
+        def regroup_planes(planes):
             grouped = stage.tile([P, GROUP * P, 4], BF16, tag="grouped_c", align_bytes=64)
-            nc.vector.tensor_copy(out=grouped[:], in_=planes[:].rearrange("p t n -> p n t"))
-            return quantise(grouped[:].rearrange("p n t -> p (n t)"), pool, tag)
+            nc.vector.tensor_copy(
+                out=grouped[:].rearrange("p (c i) t -> p c t i", i=4),
+                in_=planes[:].rearrange("p t (c i) -> p c t i", i=4),
+            )
+            return grouped
 
         regrouped_of = {}
         grouped_m_of = {}
@@ -155,6 +157,7 @@ def tile_swintransformerblock_pb_t_kernel(
         mean_of = {}
         rstd_of = {}
         planes_of = {}
+        grouped_h_of = {}
         h_of = {}
         p_of = {}
         f_of = {}
@@ -163,7 +166,7 @@ def tile_swintransformerblock_pb_t_kernel(
             b, half = divmod(g, HALVES)
             if half == 0:
                 regrouped = stage.tile([P, WIN, CH], BF16, tag="regrouped")
-                nc.vector.tensor_copy(
+                nc.scalar.copy(
                     out=regrouped[:].rearrange("p c (a d) -> p c a d", d=HEAD_DIM),
                     in_=heads_of[b][:].rearrange("p a (c d) -> p c a d", d=HEAD_DIM),
                 )
@@ -183,7 +186,7 @@ def tile_swintransformerblock_pb_t_kernel(
             nc.vector.tensor_tensor(
                 out=x2[:],
                 in0=x_of[b][:, GROUP * half : GROUP * (half + 1), :],
-                in1=out_b_bc[:].unsqueeze(1).to_broadcast([P, GROUP, CH]),
+                in1=out_b_bc.unsqueeze(1).to_broadcast([P, GROUP, CH]),
                 op=ALU.add,
             )
             x2_of[g] = x2
@@ -251,7 +254,7 @@ def tile_swintransformerblock_pb_t_kernel(
         def spread(g):
             rows = stage.tile([P, GROUP, CH], F32, tag="rows")
             if g < 0:
-                norm_bank = psum_word.tile([P, P], BF16, tag="word_bank")
+                norm_bank = psum_t.tile([P, P], BF16, tag="t_bank")
                 nc.tensor.transpose(norm_bank[:], norm_rows[:], ident_bf16[:])
                 nc.vector.tensor_copy(out=norm_cols[:], in_=norm_bank[:, 0:8])
                 nc.vector.tensor_copy(out=rows[:], in_=fc1_w_sb[:])
@@ -269,21 +272,31 @@ def tile_swintransformerblock_pb_t_kernel(
                 planes_of[g] = transpose_channel_blocks(rows, norm_cols[:, 0:4], norm_cols[:, 4:8])
 
         def pack(g):
+            grouped = grouped_h_of[g][:].rearrange("p n t -> p (n t)")
             if g < 0:
-                h_of[g] = quantise_planes(planes_of[g], consts, "fc1_w")
+                h_of[g] = quantise(grouped, consts, "fc1_w")
             else:
-                h_of[g] = quantise_planes(planes_of[g], stage, "h")
+                h_of[g] = quantise(grouped, stage, "h")
 
         def gelu(g):
             b, half = divmod(g, HALVES)
             gel = stage.tile([P, GROUP, CH], F32, tag="gel")
             for j in range(GROUP):
-                nc.vector.tensor_tensor(out=gel[:, j, :], in0=f_of[g][j][:], in1=fc1_b_bc[:], op=ALU.add)
+                nc.vector.tensor_tensor(out=gel[:, j, :], in0=f_of[g][j][:], in1=fc1_b_bc, op=ALU.add)
                 nc.scalar.activation(out=gel[:, j, :], in_=gel[:, j, :], func=ACT.Gelu)
-            nc.sync.dma_start(
-                out=out_1[b].rearrange("(p u) c -> p u c", u=RUN)[:, GROUP * half : GROUP * (half + 1), :],
-                in_=gel[:],
-            )
+                nc.sync.dma_start(
+                    out=out_1[b].rearrange("(p u) c -> p u c", u=RUN)[:, GROUP * half + j, :], in_=gel[:, j, :]
+                )
+
+        ones = consts.tile([P, P], BF16)
+        nc.vector.memset(ones[:], 1.0)
+        bias_bc = consts.tile([P, 2, CH], BF16)
+        for i in range(2):
+            bias_bank = psum_t.tile([P, CH], F32, tag="t_bank")
+            nc.tensor.matmul(out=bias_bank[:], lhsT=ones[:], rhs=bias_rows[:, i, :], start=True, stop=True)
+            nc.scalar.copy(out=bias_bc[:, i, :], in_=bias_bank[:])
+        out_b_bc = bias_bc[:, 0, :]
+        fc1_b_bc = bias_bc[:, 1, :]
 
         out_w_words = out_w_sb[:].bitcast(F32)
         out_w_packed = quantise(
@@ -305,9 +318,11 @@ def tile_swintransformerblock_pb_t_kernel(
             if live(step + 2):
                 add_bias_to_x(step + 2)
             if -1 <= step - 2 < GROUPS:
-                pack(step - 2)
+                grouped_h_of[step - 2] = regroup_planes(planes_of[step - 2])
             if live(step + 1):
                 m_of[step + 1] = quantise(grouped_m_of[step + 1][:], stage, "m")
+            if -1 <= step - 2 < GROUPS:
+                pack(step - 2)
             if live(step - 3):
                 gelu(step - 3)
             if live(step + 1):

@@ -315,12 +315,12 @@ def tile_swintransformerblock_pb_t_kernel(
                 transpose_heads(step + 2)
             if -1 <= step - 1 < GROUPS:
                 spread(step - 1)
-            if live(step + 2):
-                add_bias_to_x(step + 2)
-            if -1 <= step - 2 < GROUPS:
-                grouped_h_of[step - 2] = regroup_planes(planes_of[step - 2])
             if live(step + 1):
                 m_of[step + 1] = quantise(grouped_m_of[step + 1][:], stage, "m")
+            if -1 <= step - 2 < GROUPS:
+                grouped_h_of[step - 2] = regroup_planes(planes_of[step - 2])
+            if live(step + 2):
+                add_bias_to_x(step + 2)
             if -1 <= step - 2 < GROUPS:
                 pack(step - 2)
             if live(step - 3):

@@ -45,7 +45,7 @@ def tile_swintransformerblock_pb_t_kernel(
         heads_of = {}
         x_of = {}
 
-        def load_image(b):
+        def load_heads(b):
             heads = inputs.tile([P, HEADS, WIN * HEAD_DIM], BF16, name="heads%d" % b)
             for a in range(HEADS):
                 nc.sync.dma_start(
@@ -55,6 +55,8 @@ def tile_swintransformerblock_pb_t_kernel(
                     ),
                 )
             heads_of[b] = heads
+
+        def load_x(b):
             x_sb = inputs.tile([P, RUN, CH], BF16, name="x%d" % b)
             nc.sync.dma_start(out=x_sb[:], in_=x[b].rearrange("(p u) c -> p u c", u=RUN))
             x_of[b] = x_sb
@@ -63,18 +65,20 @@ def tile_swintransformerblock_pb_t_kernel(
         nc.vector.memset(norm_rows[:], 0.0)
         bias_rows = consts.tile([P, 2, CH], BF16)
         nc.vector.memset(bias_rows[:], 0.0)
-        nc.sync.dma_start(out=bias_rows[0:1, 0, :], in_=out_b.unsqueeze(0))
-        nc.sync.dma_start(out=bias_rows[0:1, 1, :], in_=fc1_b.unsqueeze(0))
 
         out_w_sb = consts.tile([P, 4, CH], BF16)
         nc.sync.dma_start(out=out_w_sb[:], in_=out_w.rearrange("(o p) k -> p o k", p=P))
-        load_image(0)
+        load_heads(0)
+        nc.sync.dma_start(out=bias_rows[0:1, 0, :], in_=out_b.unsqueeze(0))
+        nc.sync.dma_start(out=bias_rows[0:1, 1, :], in_=fc1_b.unsqueeze(0))
+        load_x(0)
         fc1_w_sb = consts.tile([P, 4, CH], BF16)
         nc.sync.dma_start(out=fc1_w_sb[:], in_=fc1_w.rearrange("(o p) k -> p o k", p=P))
         nc.sync.dma_start(out=norm_rows[0:4, :], in_=norm2_w.rearrange("(t p) -> t p", p=P))
         nc.sync.dma_start(out=norm_rows[4:8, :], in_=norm2_b.rearrange("(t p) -> t p", p=P))
         for b in range(1, IMAGES):
-            load_image(b)
+            load_heads(b)
+            load_x(b)
 
         ident_f32 = consts.tile([P, P], F32)
         make_identity(nc, ident_f32[:])
@@ -164,19 +168,23 @@ def tile_swintransformerblock_pb_t_kernel(
 
         def regroup_heads(g):
             b, half = divmod(g, HALVES)
-            if half == 0:
-                regrouped = stage.tile([P, WIN, CH], BF16, tag="regrouped")
-                nc.scalar.copy(
-                    out=regrouped[:].rearrange("p c (a d) -> p c a d", d=HEAD_DIM),
-                    in_=heads_of[b][:].rearrange("p a (c d) -> p c a d", d=HEAD_DIM),
-                )
-                regrouped_of[b] = regrouped
+            regrouped = stage.tile([P, GROUP, CH], BF16, tag="regrouped")
+            by_column = heads_of[b][:].rearrange("p a (c d) -> p c a d", d=HEAD_DIM)
+            first = (GROUP * half - SHIFT) % WIN
+            before_wrap = min(GROUP, WIN - first)
+            for j0, c0, count in ((0, first, before_wrap), (before_wrap, 0, GROUP - before_wrap)):
+                if count > 0:
+                    nc.scalar.copy(
+                        out=regrouped[:, j0 : j0 + count, :].rearrange("p c (a d) -> p c a d", d=HEAD_DIM),
+                        in_=by_column[:, c0 : c0 + count],
+                    )
+            regrouped_of[g] = regrouped
 
         def transpose_heads(g):
-            b, half = divmod(g, HALVES)
-            words = regrouped_of[b][:].bitcast(F32)
+            half = g % HALVES
+            words = regrouped_of[g][:].bitcast(F32)
             grouped_m_of[g] = transpose_words(
-                lambda j: words[:, (GROUP * half + j - SHIFT) % WIN, :],
+                lambda j: words[:, j, :],
                 lambda j: perm_carry[:] if GROUP * half + j < SHIFT else perm_plain[:],
             )
 
@@ -288,6 +296,16 @@ def tile_swintransformerblock_pb_t_kernel(
                     out=out_1[b].rearrange("(p u) c -> p u c", u=RUN)[:, GROUP * half + j, :], in_=gel[:, j, :]
                 )
 
+        out_w_words = out_w_sb[:].bitcast(F32)
+        out_w_packed = quantise(
+            transpose_words(lambda j: out_w_words[:, j, :], lambda j: ident_f32[:])[:], consts, "out_w"
+        )
+
+        def live(g):
+            return 0 <= g < GROUPS
+
+        regroup_heads(0)
+
         ones = consts.tile([P, P], BF16)
         nc.vector.memset(ones[:], 1.0)
         bias_bc = consts.tile([P, 2, CH], BF16)
@@ -298,15 +316,8 @@ def tile_swintransformerblock_pb_t_kernel(
         out_b_bc = bias_bc[:, 0, :]
         fc1_b_bc = bias_bc[:, 1, :]
 
-        out_w_words = out_w_sb[:].bitcast(F32)
-        out_w_packed = quantise(
-            transpose_words(lambda j: out_w_words[:, j, :], lambda j: ident_f32[:])[:], consts, "out_w"
-        )
 
-        def live(g):
-            return 0 <= g < GROUPS
-
-        for step in range(-3, GROUPS + 3):
+        for step in range(-2, GROUPS + 3):
             if live(step):
                 residual(step)
             if live(step - 3):

@@ -58,7 +58,10 @@ def tile_swintransformerblock_pb_t_kernel(
 
         def load_x(b):
             x_sb = inputs.tile([P, RUN, CH], BF16, name="x%d" % b)
-            nc.sync.dma_start(out=x_sb[:], in_=x[b].rearrange("(p u) c -> p u c", u=RUN))
+            x_rows = x[b].rearrange("(p u) c -> p u c", u=RUN)
+            for half in range(HALVES):
+                run = slice(GROUP * half, GROUP * (half + 1))
+                nc.sync.dma_start(out=x_sb[:, run, :], in_=x_rows[:, run, :])
             x_of[b] = x_sb
 
         norm_rows = consts.tile([P, P], BF16)
@@ -102,10 +105,6 @@ def tile_swintransformerblock_pb_t_kernel(
 
         minus_half = consts.tile([P, GROUP], F32)
         nc.vector.memset(minus_half[:], -0.5)
-        ones4 = consts.tile([P, 4], F32)
-        nc.vector.memset(ones4[:], 1.0)
-        zeros4 = consts.tile([P, 4], F32)
-        nc.vector.memset(zeros4[:], 0.0)
         norm_cols = consts.tile([P, 8], F32)
 
         def quantise(grouped, pool, tag):
@@ -169,13 +168,18 @@ def tile_swintransformerblock_pb_t_kernel(
         def regroup_heads(g):
             b, half = divmod(g, HALVES)
             regrouped = stage.tile([P, GROUP, CH], BF16, tag="regrouped")
-            by_column = heads_of[b][:].rearrange("p a (c d) -> p c a d", d=HEAD_DIM)
+            by_column = heads_of[b][:].rearrange("p a w -> p (a w)").bitcast(F32).rearrange(
+                "p (a c d) -> p c a d", a=HEADS, d=HEAD_DIM // 2
+            )
+            regrouped_words = regrouped[:].rearrange("p c w -> p (c w)").bitcast(F32).rearrange(
+                "p (c a d) -> p c a d", a=HEADS, d=HEAD_DIM // 2
+            )
             first = (GROUP * half - SHIFT) % WIN
             before_wrap = min(GROUP, WIN - first)
             for j0, c0, count in ((0, first, before_wrap), (before_wrap, 0, GROUP - before_wrap)):
                 if count > 0:
                     nc.scalar.copy(
-                        out=regrouped[:, j0 : j0 + count, :].rearrange("p c (a d) -> p c a d", d=HEAD_DIM),
+                        out=regrouped_words[:, j0 : j0 + count],
                         in_=by_column[:, c0 : c0 + count],
                     )
             regrouped_of[g] = regrouped
@@ -259,15 +263,21 @@ def tile_swintransformerblock_pb_t_kernel(
             mean_of[g] = neg_mean
             rstd_of[g] = rstd
 
+        def spread_weights():
+            norm_bank = psum_t.tile([P, P], BF16, tag="t_bank")
+            nc.tensor.transpose(norm_bank[:], norm_rows[:], ident_bf16[:])
+            nc.vector.tensor_copy(out=norm_cols[:], in_=norm_bank[:, 0:8])
+            grouped = stage.tile([P, GROUP * P, 4], BF16, tag="grouped_c", align_bytes=64)
+            for o in range(4):
+                bank = psum_t.tile([P, 4, P], BF16, tag="t_bank")
+                for t in range(4):
+                    nc.tensor.transpose(bank[:, t, :], fc1_w_sb[:, o, P * t : P * (t + 1)], ident_bf16[:])
+                nc.scalar.copy(out=grouped[:, P * o : P * (o + 1), :], in_=bank[:].rearrange("p t n -> p n t"))
+            grouped_h_of[-1] = grouped
+
         def spread(g):
             rows = stage.tile([P, GROUP, CH], F32, tag="rows")
-            if g < 0:
-                norm_bank = psum_t.tile([P, P], BF16, tag="t_bank")
-                nc.tensor.transpose(norm_bank[:], norm_rows[:], ident_bf16[:])
-                nc.vector.tensor_copy(out=norm_cols[:], in_=norm_bank[:, 0:8])
-                nc.vector.tensor_copy(out=rows[:], in_=fc1_w_sb[:])
-                planes_of[g] = transpose_channel_blocks(rows, ones4, zeros4)
-            else:
+            if True:
                 for j in range(GROUP):
                     nc.vector.tensor_scalar(
                         out=rows[:, j, :],
@@ -324,11 +334,13 @@ def tile_swintransformerblock_pb_t_kernel(
                 f_of[step - 3] = multiply(h_of[step - 3], h_of[-1])
             if live(step + 2):
                 transpose_heads(step + 2)
-            if -1 <= step - 1 < GROUPS:
+            if step == 0:
+                spread_weights()
+            if live(step - 1):
                 spread(step - 1)
             if live(step + 1):
                 m_of[step + 1] = quantise(grouped_m_of[step + 1][:], stage, "m")
-            if -1 <= step - 2 < GROUPS:
+            if live(step - 2):
                 grouped_h_of[step - 2] = regroup_planes(planes_of[step - 2])
             if live(step + 2):
                 add_bias_to_x(step + 2)

@@ -147,9 +147,13 @@ def tile_swintransformerblock_pb_t_kernel(
 
         def regroup_planes(planes):
             grouped = stage.tile([P, GROUP * P, 4], BF16, tag="grouped_c", align_bytes=64)
-            nc.vector.tensor_copy(
+            nc.gpsimd.tensor_scalar(
                 out=grouped[:].rearrange("p (c i) t -> p c t i", i=4),
-                in_=planes[:].rearrange("p t (c i) -> p c t i", i=4),
+                in0=planes[:].rearrange("p t (c i) -> p c t i", i=4),
+                scalar1=1.0,
+                scalar2=0.0,
+                op0=ALU.mult,
+                op1=ALU.add,
             )
             return grouped
 
@@ -231,9 +235,9 @@ def tile_swintransformerblock_pb_t_kernel(
             for j in range(GROUP):
                 nc.vector.scalar_tensor_tensor(
                     out=x2[:, j, :],
-                    in0=p_of[g][j][:],
+                    in0=x2[:, j, :],
                     scalar=1.0,
-                    in1=x2[:, j, :],
+                    in1=p_of[g][j][:],
                     op0=ALU.mult,
                     op1=ALU.add,
                     accum_out=row_sum[:, j : j + 1],
@@ -300,7 +304,7 @@ def tile_swintransformerblock_pb_t_kernel(
             b, half = divmod(g, HALVES)
             gel = stage.tile([P, GROUP, CH], F32, tag="gel")
             for j in range(GROUP):
-                nc.vector.tensor_tensor(out=gel[:, j, :], in0=f_of[g][j][:], in1=fc1_b_bc, op=ALU.add)
+                nc.vector.tensor_tensor(out=gel[:, j, :], in0=fc1_b_bc, in1=f_of[g][j][:], op=ALU.add)
                 nc.scalar.activation(out=gel[:, j, :], in_=gel[:, j, :], func=ACT.Gelu)
                 nc.sync.dma_start(
                     out=out_1[b].rearrange("(p u) c -> p u c", u=RUN)[:, GROUP * half + j, :], in_=gel[:, j, :]
@@ -338,10 +342,9 @@ def tile_swintransformerblock_pb_t_kernel(
                 spread_weights()
             if live(step - 1):
                 spread(step - 1)
+                grouped_h_of[step - 1] = regroup_planes(planes_of[step - 1])
             if live(step + 1):
                 m_of[step + 1] = quantise(grouped_m_of[step + 1][:], stage, "m")
-            if live(step - 2):
-                grouped_h_of[step - 2] = regroup_planes(planes_of[step - 2])
             if live(step + 2):
                 add_bias_to_x(step + 2)
             if -1 <= step - 2 < GROUPS:

@@ -172,19 +172,18 @@ def tile_swintransformerblock_pb_t_kernel(
         def regroup_heads(g):
             b, half = divmod(g, HALVES)
             regrouped = stage.tile([P, GROUP, CH], BF16, tag="regrouped")
-            by_column = heads_of[b][:].rearrange("p a w -> p (a w)").bitcast(F32).rearrange(
-                "p (a c d) -> p c a d", a=HEADS, d=HEAD_DIM // 2
-            )
-            regrouped_words = regrouped[:].rearrange("p c w -> p (c w)").bitcast(F32).rearrange(
-                "p (c a d) -> p c a d", a=HEADS, d=HEAD_DIM // 2
-            )
+            by_column = heads_of[b][:].rearrange("p a (c d) -> p c a d", d=HEAD_DIM)
             first = (GROUP * half - SHIFT) % WIN
             before_wrap = min(GROUP, WIN - first)
             for j0, c0, count in ((0, first, before_wrap), (before_wrap, 0, GROUP - before_wrap)):
                 if count > 0:
-                    nc.scalar.copy(
-                        out=regrouped_words[:, j0 : j0 + count],
-                        in_=by_column[:, c0 : c0 + count],
+                    nc.gpsimd.tensor_scalar(
+                        out=regrouped[:, j0 : j0 + count, :].rearrange("p c (a d) -> p c a d", d=HEAD_DIM),
+                        in0=by_column[:, c0 : c0 + count],
+                        scalar1=1.0,
+                        scalar2=0.0,
+                        op0=ALU.mult,
+                        op1=ALU.add,
                     )
             regrouped_of[g] = regrouped
 
@@ -332,6 +331,8 @@ def tile_swintransformerblock_pb_t_kernel(
 
 
         for step in range(-2, GROUPS + 3):
+            if live(step + 3):
+                regroup_heads(step + 3)
             if live(step):
                 residual(step)
             if live(step - 3):
@@ -353,5 +354,3 @@ def tile_swintransformerblock_pb_t_kernel(
                 gelu(step - 3)
             if live(step + 1):
                 p_of[step + 1] = multiply(m_of[step + 1], out_w_packed)
-            if live(step + 3):
-                regroup_heads(step + 3)

@@ -148,8 +148,8 @@ def tile_swintransformerblock_pb_t_kernel(
         def regroup_planes(planes):
             grouped = stage.tile([P, GROUP * P, 4], BF16, tag="grouped_c", align_bytes=64)
             nc.gpsimd.tensor_scalar(
-                out=grouped[:].rearrange("p (c i) t -> p c t i", i=4),
-                in0=planes[:].rearrange("p t (c i) -> p c t i", i=4),
+                out=grouped[:],
+                in0=planes[:].rearrange("p t n -> p n t"),
                 scalar1=1.0,
                 scalar2=0.0,
                 op0=ALU.mult,

@@ -38,7 +38,8 @@ def tile_swintransformerblock_pb_t_kernel(
         stage = pools.enter_context(tc.tile_pool(name="stage", bufs=2))
         rows4 = pools.enter_context(tc.tile_pool(name="rows4", bufs=5))
         stats = pools.enter_context(tc.tile_pool(name="stats", bufs=3))
-        psum_t = pools.enter_context(tc.psum_pool(name="psum_t", bufs=4))
+        psum_t = pools.enter_context(tc.psum_pool(name="psum_t", bufs=3))
+        psum_keep = pools.enter_context(tc.psum_pool(name="psum_keep", bufs=1))
         psum_acc = pools.enter_context(tc.psum_pool(name="psum_acc", bufs=4))
         pools.enter_context(tc.manual_schedule())
 
@@ -71,9 +72,9 @@ def tile_swintransformerblock_pb_t_kernel(
 
         out_w_sb = consts.tile([P, 4, CH], BF16)
         nc.sync.dma_start(out=out_w_sb[:], in_=out_w.rearrange("(o p) k -> p o k", p=P))
-        load_heads(0)
         nc.sync.dma_start(out=bias_rows[0:1, 0, :], in_=out_b.unsqueeze(0))
         nc.sync.dma_start(out=bias_rows[0:1, 1, :], in_=fc1_b.unsqueeze(0))
+        load_heads(0)
         load_x(0)
         fc1_w_sb = consts.tile([P, 4, CH], BF16)
         nc.sync.dma_start(out=fc1_w_sb[:], in_=fc1_w.rearrange("(o p) k -> p o k", p=P))
@@ -168,6 +169,7 @@ def tile_swintransformerblock_pb_t_kernel(
         h_of = {}
         p_of = {}
         f_of = {}
+        rows_of = {}
 
         def regroup_heads(g):
             b, half = divmod(g, HALVES)
@@ -201,7 +203,7 @@ def tile_swintransformerblock_pb_t_kernel(
             nc.vector.tensor_tensor(
                 out=x2[:],
                 in0=x_of[b][:, GROUP * half : GROUP * (half + 1), :],
-                in1=out_b_bc.unsqueeze(1).to_broadcast([P, GROUP, CH]),
+                in1=out_b_bank[:].unsqueeze(1).to_broadcast([P, GROUP, CH]),
                 op=ALU.add,
             )
             x2_of[g] = x2
@@ -278,19 +280,21 @@ def tile_swintransformerblock_pb_t_kernel(
                 nc.scalar.copy(out=grouped[:, P * o : P * (o + 1), :], in_=bank[:].rearrange("p t n -> p n t"))
             grouped_h_of[-1] = grouped
 
-        def spread(g):
+        def normalise(g):
             rows = stage.tile([P, GROUP, CH], F32, tag="rows")
-            if True:
-                for j in range(GROUP):
-                    nc.vector.tensor_scalar(
-                        out=rows[:, j, :],
-                        in0=x2_of[g][:, j, :],
-                        scalar1=mean_of[g][:, j : j + 1],
-                        scalar2=rstd_of[g][:, j : j + 1],
-                        op0=ALU.add,
-                        op1=ALU.mult,
-                    )
-                planes_of[g] = transpose_channel_blocks(rows, norm_cols[:, 0:4], norm_cols[:, 4:8])
+            for j in range(GROUP):
+                nc.vector.tensor_scalar(
+                    out=rows[:, j, :],
+                    in0=x2_of[g][:, j, :],
+                    scalar1=mean_of[g][:, j : j + 1],
+                    scalar2=rstd_of[g][:, j : j + 1],
+                    op0=ALU.add,
+                    op1=ALU.mult,
+                )
+            rows_of[g] = rows
+
+        def spread(g):
+            planes_of[g] = transpose_channel_blocks(rows_of[g], norm_cols[:, 0:4], norm_cols[:, 4:8])
 
         def pack(g):
             grouped = grouped_h_of[g][:].rearrange("p n t -> p (n t)")
@@ -309,6 +313,16 @@ def tile_swintransformerblock_pb_t_kernel(
                     out=out_1[b].rearrange("(p u) c -> p u c", u=RUN)[:, GROUP * half + j, :], in_=gel[:, j, :]
                 )
 
+        ones = consts.tile([P, P], BF16)
+        nc.vector.memset(ones[:], 1.0)
+        out_b_bank = psum_keep.tile([P, CH], F32)
+        nc.tensor.matmul(out=out_b_bank[:], lhsT=ones[:], rhs=bias_rows[:, 0, :], start=True, stop=True)
+        fc1_b_bank = psum_t.tile([P, CH], F32, tag="t_bank")
+        nc.tensor.matmul(out=fc1_b_bank[:], lhsT=ones[:], rhs=bias_rows[:, 1, :], start=True, stop=True)
+        fc1_b_sb = consts.tile([P, CH], BF16)
+        nc.scalar.copy(out=fc1_b_sb[:], in_=fc1_b_bank[:])
+        fc1_b_bc = fc1_b_sb[:]
+
         out_w_words = out_w_sb[:].bitcast(F32)
         out_w_packed = quantise(
             transpose_words(lambda j: out_w_words[:, j, :], lambda j: ident_f32[:])[:], consts, "out_w"
@@ -319,24 +333,16 @@ def tile_swintransformerblock_pb_t_kernel(
 
         regroup_heads(0)
 
-        ones = consts.tile([P, P], BF16)
-        nc.vector.memset(ones[:], 1.0)
-        bias_bc = consts.tile([P, 2, CH], BF16)
-        for i in range(2):
-            bias_bank = psum_t.tile([P, CH], F32, tag="t_bank")
-            nc.tensor.matmul(out=bias_bank[:], lhsT=ones[:], rhs=bias_rows[:, i, :], start=True, stop=True)
-            nc.scalar.copy(out=bias_bc[:, i, :], in_=bias_bank[:])
-        out_b_bc = bias_bc[:, 0, :]
-        fc1_b_bc = bias_bc[:, 1, :]
-
 
         for step in range(-2, GROUPS + 3):
-            if live(step + 3):
-                regroup_heads(step + 3)
             if live(step):
                 residual(step)
+            if live(step + 3):
+                regroup_heads(step + 3)
             if live(step - 3):
                 f_of[step - 3] = multiply(h_of[step - 3], h_of[-1])
+            if live(step - 1):
+                normalise(step - 1)
             if live(step + 2):
                 transpose_heads(step + 2)
             if step == 0:
@@ -346,11 +352,13 @@ def tile_swintransformerblock_pb_t_kernel(
                 grouped_h_of[step - 1] = regroup_planes(planes_of[step - 1])
             if live(step + 1):
                 m_of[step + 1] = quantise(grouped_m_of[step + 1][:], stage, "m")
+            if -1 <= step - 2 < GROUPS and step < GROUPS:
+                pack(step - 2)
             if live(step + 2):
                 add_bias_to_x(step + 2)
-            if -1 <= step - 2 < GROUPS:
-                pack(step - 2)
             if live(step - 3):
                 gelu(step - 3)
+            if -1 <= step - 2 < GROUPS and step >= GROUPS:
+                pack(step - 2)
             if live(step + 1):
                 p_of[step + 1] = multiply(m_of[step + 1], out_w_packed)

@@ -174,19 +174,17 @@ def tile_swintransformerblock_pb_t_kernel(
         def regroup_heads(g):
             b, half = divmod(g, HALVES)
             regrouped = stage.tile([P, GROUP, CH], BF16, tag="regrouped")
-            by_column = heads_of[b][:].rearrange("p a (c d) -> p c a d", d=HEAD_DIM)
+            by_column = heads_of[b][:].rearrange("p a w -> p (a w)").bitcast(F32).rearrange(
+                "p (a c d) -> p c a d", a=HEADS, d=HEAD_DIM // 2
+            )
+            regrouped_words = regrouped[:].rearrange("p c w -> p (c w)").bitcast(F32).rearrange(
+                "p (c a d) -> p c a d", a=HEADS, d=HEAD_DIM // 2
+            )
             first = (GROUP * half - SHIFT) % WIN
             before_wrap = min(GROUP, WIN - first)
             for j0, c0, count in ((0, first, before_wrap), (before_wrap, 0, GROUP - before_wrap)):
                 if count > 0:
-                    nc.gpsimd.tensor_scalar(
-                        out=regrouped[:, j0 : j0 + count, :].rearrange("p c (a d) -> p c a d", d=HEAD_DIM),
-                        in0=by_column[:, c0 : c0 + count],
-                        scalar1=1.0,
-                        scalar2=0.0,
-                        op0=ALU.mult,
-                        op1=ALU.add,
-                    )
+                    nc.scalar.copy(out=regrouped_words[:, j0 : j0 + count], in_=by_column[:, c0 : c0 + count])
             regrouped_of[g] = regrouped
 
         def transpose_heads(g):
@@ -337,8 +335,6 @@ def tile_swintransformerblock_pb_t_kernel(
         for step in range(-2, GROUPS + 3):
             if live(step):
                 residual(step)
-            if live(step + 3):
-                regroup_heads(step + 3)
             if live(step - 3):
                 f_of[step - 3] = multiply(h_of[step - 3], h_of[-1])
             if live(step - 1):
@@ -356,6 +352,8 @@ def tile_swintransformerblock_pb_t_kernel(
                 pack(step - 2)
             if live(step + 2):
                 add_bias_to_x(step + 2)
+            if live(step + 3):
+                regroup_heads(step + 3)
             if live(step - 3):
                 gelu(step - 3)
             if -1 <= step - 2 < GROUPS and step >= GROUPS:

@@ -305,11 +305,18 @@ def tile_swintransformerblock_pb_t_kernel(
             b, half = divmod(g, HALVES)
             gel = stage.tile([P, GROUP, CH], F32, tag="gel")
             for j in range(GROUP):
-                nc.vector.tensor_tensor(out=gel[:, j, :], in0=fc1_b_bc, in1=f_of[g][j][:], op=ALU.add)
-                nc.scalar.activation(out=gel[:, j, :], in_=gel[:, j, :], func=ACT.Gelu)
-                nc.sync.dma_start(
-                    out=out_1[b].rearrange("(p u) c -> p u c", u=RUN)[:, GROUP * half + j, :], in_=gel[:, j, :]
-                )
+                pieces = 2 if (g == GROUPS - 1 and j == GROUP - 1) else 1
+                width = CH // pieces
+                for piece in range(pieces):
+                    cols = slice(width * piece, width * (piece + 1))
+                    nc.vector.tensor_tensor(
+                        out=gel[:, j, cols], in0=fc1_b_bc[:, cols], in1=f_of[g][j][:, cols], op=ALU.add
+                    )
+                    nc.scalar.activation(out=gel[:, j, cols], in_=gel[:, j, cols], func=ACT.Gelu)
+                    nc.sync.dma_start(
+                        out=out_1[b].rearrange("(p u) c -> p u c", u=RUN)[:, GROUP * half + j, cols],
+                        in_=gel[:, j, cols],
+                    )
 
         ones = consts.tile([P, P], BF16)
         nc.vector.memset(ones[:], 1.0)

from contextlib import ExitStack

import concourse.mybir as mybir
from concourse.masks import make_identity

F32 = mybir.dt.float32
BF16 = mybir.dt.bfloat16
U32 = mybir.dt.uint32
U8 = mybir.dt.uint8
FP8X4 = mybir.dt.float8_e4m3fn_x4
ALU = mybir.AluOpType
ACT = mybir.ActivationFunctionType

P = 128
IMAGES = 4
CH = 512
HEADS = 16
HEAD_DIM = 32
WIN = 8
WINDOWS = 16
SHIFT = 3
RUN = 8
GROUP = 4
HALVES = RUN // GROUP
GROUPS = IMAGES * HALVES
EPS = 1e-5

FLOPS = 2 * 2 * IMAGES * 1024 * CH * CH


def tile_swintransformerblock_pb_t_kernel(
    tc, o_heads, x, out_w, out_b, norm2_w, norm2_b, fc1_w, fc1_b, out_0, out_1
):
    nc = tc.nc
    with ExitStack() as pools:
        consts = pools.enter_context(tc.tile_pool(name="consts", bufs=1))
        inputs = pools.enter_context(tc.tile_pool(name="inputs", bufs=1))
        stage = pools.enter_context(tc.tile_pool(name="stage", bufs=2))
        rows4 = pools.enter_context(tc.tile_pool(name="rows4", bufs=5))
        stats = pools.enter_context(tc.tile_pool(name="stats", bufs=3))
        psum_t = pools.enter_context(tc.psum_pool(name="psum_t", bufs=3))
        psum_keep = pools.enter_context(tc.psum_pool(name="psum_keep", bufs=1))
        psum_acc = pools.enter_context(tc.psum_pool(name="psum_acc", bufs=4))
        pools.enter_context(tc.manual_schedule())

        heads_of = {}
        x_of = {}

        def load_heads(b):
            heads = inputs.tile([P, HEADS, WIN * HEAD_DIM], BF16, name="heads%d" % b)
            for a in range(HEADS):
                nc.sync.dma_start(
                    out=heads[:, a, :],
                    in_=o_heads[WINDOWS * b : WINDOWS * (b + 1), a].rearrange(
                        "n (r c) d -> n r (c d)", c=WIN
                    ),
                )
            heads_of[b] = heads

        def load_x(b):
            x_sb = inputs.tile([P, RUN, CH], BF16, name="x%d" % b)
            x_rows = x[b].rearrange("(p u) c -> p u c", u=RUN)
            for half in range(HALVES):
                run = slice(GROUP * half, GROUP * (half + 1))
                nc.sync.dma_start(out=x_sb[:, run, :], in_=x_rows[:, run, :])
            x_of[b] = x_sb

        norm_rows = consts.tile([P, P], BF16)
        nc.vector.memset(norm_rows[:], 0.0)
        bias_rows = consts.tile([P, 2, CH], BF16)
        nc.vector.memset(bias_rows[:], 0.0)

        out_w_sb = consts.tile([P, 4, CH], BF16)
        nc.sync.dma_start(out=out_w_sb[:], in_=out_w.rearrange("(o p) k -> p o k", p=P))
        nc.sync.dma_start(out=bias_rows[0:1, 0, :], in_=out_b.unsqueeze(0))
        nc.sync.dma_start(out=bias_rows[0:1, 1, :], in_=fc1_b.unsqueeze(0))
        load_heads(0)
        load_x(0)
        fc1_w_sb = consts.tile([P, 4, CH], BF16)
        nc.sync.dma_start(out=fc1_w_sb[:], in_=fc1_w.rearrange("(o p) k -> p o k", p=P))
        nc.sync.dma_start(out=norm_rows[0:4, :], in_=norm2_w.rearrange("(t p) -> t p", p=P))
        nc.sync.dma_start(out=norm_rows[4:8, :], in_=norm2_b.rearrange("(t p) -> t p", p=P))
        for b in range(1, IMAGES):
            load_heads(b)
            load_x(b)

        ident_f32 = consts.tile([P, P], F32)
        make_identity(nc, ident_f32[:])
        ident_bf16 = consts.tile([P, P], BF16)
        make_identity(nc, ident_bf16[:])

        row_major = consts.tile([P, P], F32)
        nc.vector.tensor_copy(
            out=row_major[:].rearrange("k (wi r wj) -> k wi r wj", wi=4, r=WIN),
            in_=ident_f32[:].rearrange("k (wi wj r) -> k wi r wj", wi=4, wj=4),
        )
        perm_plain = consts.tile([P, P], F32)
        roll = 4 * SHIFT
        nc.vector.tensor_copy(out=perm_plain[:, roll:P], in_=row_major[:, 0 : P - roll])
        nc.vector.tensor_copy(out=perm_plain[:, 0:roll], in_=row_major[:, P - roll : P])
        perm_carry = consts.tile([P, P], F32)
        plain_v = perm_plain[:].rearrange("k (i q) -> k i q", q=4)
        carry_v = perm_carry[:].rearrange("k (i q) -> k i q", q=4)
        nc.vector.tensor_copy(out=carry_v[:, :, 1:4], in_=plain_v[:, :, 0:3])
        nc.vector.tensor_copy(out=carry_v[:, :, 0:1], in_=plain_v[:, :, 3:4])

        minus_half = consts.tile([P, GROUP], F32)
        nc.vector.memset(minus_half[:], -0.5)
        norm_cols = consts.tile([P, 8], F32)

        def quantise(grouped, pool, tag):
            codes = pool.tile([P, GROUP * P], U32, tag=tag + "_codes", name=tag + "_codes", align_bytes=64)
            scales = pool.tile([P, GROUP * P], U8, tag=tag + "_scales", name=tag + "_scales", align_bytes=64)
            nc.vector.quantize_mx(out=codes[:].bitcast(FP8X4), scales=scales[:], in_=grouped)
            return codes, scales

        def transpose_words(words_of, perm_of):
            grouped = stage.tile([P, GROUP * P * 4], BF16, tag="grouped_w", align_bytes=64)
            grouped_words = grouped[:].bitcast(F32).rearrange("w (n h) -> w n h", h=2)
            for pair in range(GROUP // 2):
                bank = psum_t.tile([P, 2, 2, P], F32, tag="t_bank")
                for h in range(2):
                    for jj in range(2):
                        j = 2 * pair + jj
                        nc.tensor.transpose(
                            bank[:, h, jj, :], words_of(j)[:, P * h : P * (h + 1)], perm_of(j)
                        )
                nc.scalar.copy(
                    out=grouped_words[:, 2 * P * pair : 2 * P * (pair + 1), :],
                    in_=bank[:].rearrange("w h j n -> w (j n) h"),
                )
            return grouped

        def transpose_channel_blocks(rows, gain, beta):
            planes = stage.tile([P, 4, GROUP * P], BF16, tag="planes")
            for t in range(4):
                bank = psum_t.tile([P, GROUP, P], F32, tag="t_bank")
                for j in range(GROUP):
                    nc.tensor.transpose(bank[:, j, :], rows[:, j, P * t : P * (t + 1)], ident_f32[:])
                nc.scalar.activation(
                    out=planes[:, t, :],
                    in_=bank[:].rearrange("p j n -> p (j n)"),
                    func=ACT.Identity,
                    scale=gain[:, t : t + 1],
                    bias=beta[:, t : t + 1],
                )
            return planes

        def regroup_planes(planes):
            grouped = stage.tile([P, GROUP * P, 4], BF16, tag="grouped_c", align_bytes=64)
            nc.gpsimd.tensor_scalar(
                out=grouped[:],
                in0=planes[:].rearrange("p t n -> p n t"),
                scalar1=1.0,
                scalar2=0.0,
                op0=ALU.mult,
                op1=ALU.add,
            )
            return grouped

        regrouped_of = {}
        grouped_m_of = {}
        m_of = {}
        x2_of = {}
        mean_of = {}
        rstd_of = {}
        planes_of = {}
        grouped_h_of = {}
        h_of = {}
        p_of = {}
        f_of = {}
        rows_of = {}

        def regroup_heads(g):
            b, half = divmod(g, HALVES)
            regrouped = stage.tile([P, GROUP, CH], BF16, tag="regrouped")
            by_column = heads_of[b][:].rearrange("p a w -> p (a w)").bitcast(F32).rearrange(
                "p (a c d) -> p c a d", a=HEADS, d=HEAD_DIM // 2
            )
            regrouped_words = regrouped[:].rearrange("p c w -> p (c w)").bitcast(F32).rearrange(
                "p (c a d) -> p c a d", a=HEADS, d=HEAD_DIM // 2
            )
            first = (GROUP * half - SHIFT) % WIN
            before_wrap = min(GROUP, WIN - first)
            for j0, c0, count in ((0, first, before_wrap), (before_wrap, 0, GROUP - before_wrap)):
                if count > 0:
                    nc.scalar.copy(out=regrouped_words[:, j0 : j0 + count], in_=by_column[:, c0 : c0 + count])
            regrouped_of[g] = regrouped

        def transpose_heads(g):
            half = g % HALVES
            words = regrouped_of[g][:].bitcast(F32)
            grouped_m_of[g] = transpose_words(
                lambda j: words[:, j, :],
                lambda j: perm_carry[:] if GROUP * half + j < SHIFT else perm_plain[:],
            )

        def add_bias_to_x(g):
            b, half = divmod(g, HALVES)
            x2 = rows4.tile([P, GROUP, CH], F32, tag="x2")
            nc.vector.tensor_tensor(
                out=x2[:],
                in0=x_of[b][:, GROUP * half : GROUP * (half + 1), :],
                in1=out_b_bank[:].unsqueeze(1).to_broadcast([P, GROUP, CH]),
                op=ALU.add,
            )
            x2_of[g] = x2

        def multiply(tokens, weights):
            codes, scales = tokens
            w_codes, w_scales = weights
            banks = []
            for j in range(GROUP):
                cols = slice(P * j, P * (j + 1))
                acc = psum_acc.tile([P, CH], F32, tag="acc")
                nc.tensor.matmul_mx(
                    out=acc[:],
                    lhsT=codes[:, cols].bitcast(FP8X4),
                    lhsT_scale=scales[:, cols],
                    rhs=w_codes[:].bitcast(FP8X4),
                    rhs_scale=w_scales[:],
                    start=True,
                    stop=True,
                )
                banks.append(acc)
            return banks

        def residual(g):
            b, half = divmod(g, HALVES)
            x2 = x2_of[g]
            row_sum = stats.tile([P, GROUP], F32, tag="row_sum")
            squares = stage.tile([P, GROUP, CH], BF16, tag="squares")
            sq_sum = stats.tile([P, GROUP], F32, tag="sq_sum")
            for j in range(GROUP):
                nc.vector.scalar_tensor_tensor(
                    out=x2[:, j, :],
                    in0=x2[:, j, :],
                    scalar=1.0,
                    in1=p_of[g][j][:],
                    op0=ALU.mult,
                    op1=ALU.add,
                    accum_out=row_sum[:, j : j + 1],
                )
                nc.scalar.activation(
                    out=squares[:, j, :],
                    in_=x2[:, j, :],
                    func=ACT.Square,
                    bias=row_sum[:, j : j + 1],
                    scale=-1.0 * CH,
                    accum_out=sq_sum[:, j : j + 1],
                )
            nc.sync.dma_start(
                out=out_0[b].rearrange("(p u) c -> p u c", u=RUN)[:, GROUP * half : GROUP * (half + 1), :],
                in_=x2[:],
            )
            neg_mean = stats.tile([P, GROUP], F32, tag="neg_mean")
            nc.gpsimd.tensor_scalar(
                out=neg_mean[:], in0=row_sum[:], scalar1=-1.0 / CH, scalar2=0.0, op0=ALU.mult, op1=ALU.add
            )
            var_eps = stats.tile([P, GROUP], F32, tag="var_eps")
            nc.gpsimd.tensor_scalar(
                out=var_eps[:], in0=sq_sum[:], scalar1=1.0 / CH**3, scalar2=EPS, op0=ALU.mult, op1=ALU.add
            )
            rstd = stats.tile([P, GROUP], F32, tag="rstd")
            nc.gpsimd.tensor_tensor(out=rstd[:], in0=var_eps[:], in1=minus_half[:], op=ALU.pow)
            mean_of[g] = neg_mean
            rstd_of[g] = rstd

        def spread_weights():
            norm_bank = psum_t.tile([P, P], BF16, tag="t_bank")
            nc.tensor.transpose(norm_bank[:], norm_rows[:], ident_bf16[:])
            nc.vector.tensor_copy(out=norm_cols[:], in_=norm_bank[:, 0:8])
            grouped = stage.tile([P, GROUP * P, 4], BF16, tag="grouped_c", align_bytes=64)
            for o in range(4):
                bank = psum_t.tile([P, 4, P], BF16, tag="t_bank")
                for t in range(4):
                    nc.tensor.transpose(bank[:, t, :], fc1_w_sb[:, o, P * t : P * (t + 1)], ident_bf16[:])
                nc.scalar.copy(out=grouped[:, P * o : P * (o + 1), :], in_=bank[:].rearrange("p t n -> p n t"))
            grouped_h_of[-1] = grouped

        def normalise(g):
            rows = stage.tile([P, GROUP, CH], F32, tag="rows")
            for j in range(GROUP):
                nc.vector.tensor_scalar(
                    out=rows[:, j, :],
                    in0=x2_of[g][:, j, :],
                    scalar1=mean_of[g][:, j : j + 1],
                    scalar2=rstd_of[g][:, j : j + 1],
                    op0=ALU.add,
                    op1=ALU.mult,
                )
            rows_of[g] = rows

        def spread(g):
            planes_of[g] = transpose_channel_blocks(rows_of[g], norm_cols[:, 0:4], norm_cols[:, 4:8])

        def pack(g):
            grouped = grouped_h_of[g][:].rearrange("p n t -> p (n t)")
            if g < 0:
                h_of[g] = quantise(grouped, consts, "fc1_w")
            else:
                h_of[g] = quantise(grouped, stage, "h")

        def gelu(g):
            b, half = divmod(g, HALVES)
            gel = stage.tile([P, GROUP, CH], F32, tag="gel")
            for j in range(GROUP):
                pieces = 2 if (g == GROUPS - 1 and j == GROUP - 1) else 1
                width = CH // pieces
                for piece in range(pieces):
                    cols = slice(width * piece, width * (piece + 1))
                    nc.vector.tensor_tensor(
                        out=gel[:, j, cols], in0=fc1_b_bc[:, cols], in1=f_of[g][j][:, cols], op=ALU.add
                    )
                    nc.scalar.activation(out=gel[:, j, cols], in_=gel[:, j, cols], func=ACT.Gelu)
                    nc.sync.dma_start(
                        out=out_1[b].rearrange("(p u) c -> p u c", u=RUN)[:, GROUP * half + j, cols],
                        in_=gel[:, j, cols],
                    )

        ones = consts.tile([P, P], BF16)
        nc.vector.memset(ones[:], 1.0)
        out_b_bank = psum_keep.tile([P, CH], F32)
        nc.tensor.matmul(out=out_b_bank[:], lhsT=ones[:], rhs=bias_rows[:, 0, :], start=True, stop=True)
        fc1_b_bank = psum_t.tile([P, CH], F32, tag="t_bank")
        nc.tensor.matmul(out=fc1_b_bank[:], lhsT=ones[:], rhs=bias_rows[:, 1, :], start=True, stop=True)
        fc1_b_sb = consts.tile([P, CH], BF16)
        nc.scalar.copy(out=fc1_b_sb[:], in_=fc1_b_bank[:])
        fc1_b_bc = fc1_b_sb[:]

        out_w_words = out_w_sb[:].bitcast(F32)
        out_w_packed = quantise(
            transpose_words(lambda j: out_w_words[:, j, :], lambda j: ident_f32[:])[:], consts, "out_w"
        )

        def live(g):
            return 0 <= g < GROUPS

        regroup_heads(0)


        for step in range(-2, GROUPS + 3):
            if live(step):
                residual(step)
            if live(step - 3):
                f_of[step - 3] = multiply(h_of[step - 3], h_of[-1])
            if live(step - 1):
                normalise(step - 1)
            if live(step + 2):
                transpose_heads(step + 2)
            if step == 0:
                spread_weights()
            if live(step - 1):
                spread(step - 1)
                grouped_h_of[step - 1] = regroup_planes(planes_of[step - 1])
            if live(step + 1):
                m_of[step + 1] = quantise(grouped_m_of[step + 1][:], stage, "m")
            if -1 <= step - 2 < GROUPS and step < GROUPS:
                pack(step - 2)
            if live(step + 2):
                add_bias_to_x(step + 2)
            if live(step + 3):
                regroup_heads(step + 3)
            if live(step - 3):
                gelu(step - 3)
            if -1 <= step - 2 < GROUPS and step >= GROUPS:
                pack(step - 2)
            if live(step + 1):
                p_of[step + 1] = multiply(m_of[step + 1], out_w_packed)
